import numpy as np
import ml_dtypes


def mxq(x, axis, fmt="e4m3"):
    dtype, down = {"e4m3": (ml_dtypes.float8_e4m3fn, 7), "e5m2": (ml_dtypes.float8_e5m2, 14)}[fmt]
    v = np.moveaxis(np.asarray(x, np.float32).astype(ml_dtypes.bfloat16).astype(np.float64), axis, -1)
    blocks = v.reshape(v.shape[:-1] + (-1, 32))
    amax = np.abs(blocks).max(-1, keepdims=True)
    byte = np.maximum(np.where(amax > 0, np.frexp(amax)[1] - 1 + 127, 0) - down, 1)
    scale = np.exp2(byte - 127.0)
    codes = (blocks / scale).astype(np.float32).astype(dtype).astype(np.float64)
    return np.moveaxis((codes * scale).reshape(v.shape), -1, axis)


WIDE = False


def mx_kscale(k):
    if not WIDE:
        return np.ones(k)
    levels = np.array([10, -10, 5, -5, 0])
    a = np.random.permutation(np.resize(levels, k // 512 * 4)).reshape(k // 512, 4)
    idx = np.arange(k)
    return np.exp2(a[idx // 512, idx % 128 // 32])


BF16 = ml_dtypes.bfloat16


def bf(x):
    return np.asarray(x, np.float32).astype(BF16)


def f64(x):
    return np.asarray(x).astype(np.float64)


N, E, C, D1, D2 = 1024, 2048, 512, 2, 2
T1 = D1 + 1


def shift_down(y, k):
    return np.pad(y, ((k, 0), (0, 0)))[:y.shape[0]] if k > 0 else y


def setup_inputs():
    s = mx_kscale(E)
    return {"x": bf(np.random.standard_normal((N, E)) * s),
            "W1": bf(np.random.standard_normal((T1, E, C)) * 0.4 / np.sqrt(E) / s[None, :, None]),
            "b1": bf(np.random.standard_normal((1, C)) * 0.25)}


def reference(x, W1, b1):
    Y = mxq(f64(x), 1, "e4m3") @ mxq(f64(W1), 1, "e4m3")
    S = sum(shift_down(Y[k], k) for k in range(T1))
    cnt1 = np.minimum(np.arange(N), D1) + 1.0
    return np.tanh(S + cnt1[:, None] * f64(b1)[0])

@@ -1,0 +1,183 @@
+from contextlib import ExitStack
+
+import concourse.mybir as mybir
+from concourse.masks import make_identity
+
+F32 = mybir.dt.float32
+BF16 = mybir.dt.bfloat16
+U32 = mybir.dt.uint32
+U8 = mybir.dt.uint8
+FP8X4 = mybir.dt.float8_e4m3fn_x4
+ACT = mybir.ActivationFunctionType
+ALU = mybir.AluOpType
+
+P = 128
+ROWS, E, C, TAPS = 1024, 2048, 512, 3
+TILES = ROWS // P
+SLABS = E // 512
+CHUNKS = SLABS * TAPS
+SLOTS = TILES + 2
+ARRIVAL = [6, 7, 0, 1, 2, 3, 4, 5]
+V_COLS = 256
+FLOPS = 2 * ROWS * E * C * TAPS
+PIN = False
+
+
+def slot_of(j, tap):
+    src = j - tap
+    return src if src >= 0 else src + SLOTS
+
+
+def tile_predictor_pa_kernel(tc, x, W1, b1, out):
+    nc = tc.nc
+    with ExitStack() as ctx:
+        keep = ctx.enter_context(tc.tile_pool(name="keep", bufs=1))
+        stage = ctx.enter_context(tc.tile_pool(name="stage", bufs=3))
+        psum = ctx.enter_context(tc.psum_pool(name="psum", bufs=1))
+        if PIN:
+            ctx.enter_context(tc.manual_schedule())
+
+        x_rows = x.rearrange("(i j) k -> i j k", j=TILES)
+        x_sb = {}
+        for j in ARRIVAL:
+            x_sb[j] = keep.tile([P, E], BF16, name="x_sb%d" % j)
+            nc.sync.dma_start(out=x_sb[j][:], in_=x_rows[:, j, :])
+        w_raw = []
+        for c in range(CHUNKS):
+            g, tap = divmod(c, TAPS)
+            raw = keep.tile([P, 4, C], BF16, name="w_raw%d" % c)
+            nc.sync.dma_start(
+                out=raw[:].rearrange("p (u e) c -> p u (e c)", u=2),
+                in_=W1[tap, 512 * g : 512 * (g + 1), :].rearrange("(u q e) c -> q u (e c)", u=2, e=2),
+            )
+            w_raw.append(raw)
+        bias_raw = keep.tile([P, C], BF16, name="bias_raw")
+        nc.sync.dma_start(out=bias_raw[:], in_=b1[0, :].partition_broadcast(P))
+
+        warm = keep.tile([P, 1], F32, name="warm")
+        warm_out = keep.tile([P, 1], F32, name="warm_out")
+        nc.vector.memset(warm[:], 0.0)
+        nc.scalar.activation(out=warm_out[:], in_=warm[:], func=ACT.Tanh)
+        ident = keep.tile([P, P], F32, name="ident")
+        make_identity(nc, ident[:])
+        count0 = keep.tile([P, 1], F32, name="count0")
+        count1 = keep.tile([P, 1], F32, name="count1")
+        nc.vector.memset(count0[:], 3.0)
+        nc.vector.memset(count0[0:1, :], 1.0)
+        nc.vector.memset(count1[:], 3.0)
+        nc.vector.memset(count1[0:1, :], 2.0)
+
+        xg, xg32, xc, xs = [], [], [], []
+        for g in range(SLABS):
+            grouped = keep.tile([P, SLOTS, P, 4], BF16, name="xg%d" % g, align_bytes=64)
+            nc.vector.memset(grouped[:, TILES:SLOTS, :, :], 0.0)
+            xg.append(grouped)
+            xg32.append(grouped[:].bitcast(F32))
+            xc.append(keep.tile([P, SLOTS, P], U32, name="xc%d" % g, align_bytes=64))
+            xs.append(keep.tile([P, SLOTS, P], U8, name="xs%d" % g, align_bytes=64))
+
+        def quantise_x(g, s0, s1):
+            nc.vector.quantize_mx(
+                out=xc[g][:, s0:s1, :].rearrange("p s r -> p (s r)").bitcast(FP8X4),
+                scales=xs[g][:, s0:s1, :].rearrange("p s r -> p (s r)"),
+                in_=xg[g][:, s0:s1, :, :].rearrange("p s r t -> p (s r t)"),
+            )
+
+        def shift_copy(g):
+            nc.vector.tensor_copy(
+                out=xg[g][:, TILES:SLOTS, 1:P, :].rearrange("p s r t -> p s (r t)"),
+                in_=xg[g][:, 6:8, 0 : P - 1, :].rearrange("p s r t -> p s (r t)"),
+            )
+
+        for n in range(TILES // 2):
+            j0 = ARRIVAL[2 * n]
+            banks = []
+            for g in range(SLABS):
+                banks.append(psum.tile([P, 2, 2, P], F32, tag="bank%d" % (4 * (n % 2) + g), name="tp%d_%d" % (n, g)))
+            for jj in range(2):
+                words = x_sb[j0 + jj][:].bitcast(F32)
+                for g in range(SLABS):
+                    for u in range(2):
+                        w0 = 256 * g + 128 * u
+                        nc.tensor.transpose(banks[g][:, jj, u, :], words[:, w0 : w0 + P], ident[:])
+            for g in range(SLABS):
+                copy = nc.scalar.copy if g % 2 == 0 else nc.vector.tensor_copy
+                copy(out=xg32[g][:, j0 : j0 + 2, :, :], in_=banks[g][:].rearrange("p j u r -> p j r u"))
+                if g == 1:
+                    quantise_x(0, j0, j0 + 2)
+            if n == 0:
+                shift_copy(0)
+            if n == 1:
+                quantise_x(0, TILES, SLOTS)
+
+        wc, ws, wg = [], [], {}
+        for c in range(CHUNKS):
+            wc.append(keep.tile([P, C], U32, name="wc%d" % c, align_bytes=64))
+            ws.append(keep.tile([P, C], U8, name="ws%d" % c, align_bytes=64))
+
+        def regroup(c):
+            wg[c] = stage.tile([P, C, 4], BF16, tag="wg", name="wg%d" % c, align_bytes=64)
+            for copy, c0, c1 in ((nc.vector.tensor_copy, 0, V_COLS), (nc.scalar.copy, V_COLS, C)):
+                copy(
+                    out=wg[c][:, c0:c1, :].rearrange("p (c i) t -> p c t i", i=4),
+                    in_=w_raw[c][:, :, c0:c1].rearrange("p t (c i) -> p c t i", i=4),
+                )
+
+        def quantise_w(c):
+            nc.vector.quantize_mx(
+                out=wc[c][:].bitcast(FP8X4),
+                scales=ws[c][:],
+                in_=wg[c][:].rearrange("p c t -> p (c t)"),
+            )
+
+        acc = {}
+        for pos, j in enumerate(ARRIVAL):
+            acc[j] = psum.tile([P, C], F32, tag="bank%d" % pos, name="acc%d" % j)
+
+        def mx_pass(j, c):
+            g, tap = divmod(c, TAPS)
+            s = slot_of(j, tap)
+            nc.tensor.matmul_mx(
+                out=acc[j][:],
+                lhsT=xc[g][:, s, :].bitcast(FP8X4),
+                lhsT_scale=xs[g][:, s, :],
+                rhs=wc[c][:].bitcast(FP8X4),
+                rhs_scale=ws[c][:],
+                start=(c == 0),
+                stop=(c == CHUNKS - 1),
+            )
+
+        regroup(0)
+        for c in range(CHUNKS):
+            g, tap = divmod(c, TAPS)
+            if c + 1 < CHUNKS:
+                regroup(c + 1)
+            quantise_w(c)
+            if g + 1 < SLABS:
+                if tap == 0:
+                    shift_copy(g + 1)
+                elif tap == 1:
+                    quantise_x(g + 1, 0, TILES)
+                else:
+                    quantise_x(g + 1, TILES, SLOTS)
+            if g + 1 < SLABS:
+                for j in ARRIVAL:
+                    mx_pass(j, c)
+
+        bias3 = keep.tile([P, C], F32, name="bias3")
+        bias_t0 = keep.tile([P, C], F32, name="bias_t0")
+        bias_t1 = keep.tile([P, C], F32, name="bias_t1")
+        nc.scalar.activation(out=bias3[:], in_=bias_raw[:], func=ACT.Copy, scale=3.0)
+        nc.scalar.activation(out=bias_t0[:], in_=bias_raw[:], func=ACT.Copy, scale=count0[:, 0:1])
+        nc.scalar.activation(out=bias_t1[:], in_=bias_raw[:], func=ACT.Copy, scale=count1[:, 0:1])
+        bias_of = {0: bias_t0, 1: bias_t1}
+
+        out_rows = out.rearrange("(i j) c -> i j c", j=TILES)
+        for j in ARRIVAL:
+            for tap in range(TAPS):
+                mx_pass(j, (SLABS - 1) * TAPS + tap)
+            summed = stage.tile([P, C], F32, tag="summed", name="summed%d" % j)
+            nc.vector.tensor_tensor(out=summed[:], in0=acc[j][:], in1=bias_of.get(j, bias3)[:], op=ALU.add)
+            result = stage.tile([P, C], F32, tag="result", name="result%d" % j)
+            nc.scalar.activation(out=result[:], in_=summed[:], func=ACT.Tanh)
+            nc.sync.dma_start(out=out_rows[:, j, :], in_=result[:])

@@ -18,9 +18,13 @@ SLABS = E // 512
 CHUNKS = SLABS * TAPS
 SLOTS = TILES + 2
 ARRIVAL = [6, 7, 0, 1, 2, 3, 4, 5]
-V_COLS = 256
+EARLY = ARRIVAL[:7]
+LATE = ARRIVAL[7]
+LATE_GROUPS = ((7, 0, 256), (0, 256, 384), (1, 384, 512))
+CM = 8
+V_COLS = [336, 256] + [192] * 10
 FLOPS = 2 * ROWS * E * C * TAPS
-PIN = False
+PIN = True
 
 
 def slot_of(j, tap):
@@ -51,15 +55,18 @@ def tile_predictor_pa_kernel(tc, x, W1, b1, out):
                 in_=W1[tap, 512 * g : 512 * (g + 1), :].rearrange("(u q e) c -> q u (e c)", u=2, e=2),
             )
             w_raw.append(raw)
-        bias_raw = keep.tile([P, C], BF16, name="bias_raw")
-        nc.sync.dma_start(out=bias_raw[:], in_=b1[0, :].partition_broadcast(P))
 
+        bias_row = keep.tile([P, C], BF16, name="bias_row")
+        nc.vector.memset(bias_row[:], 0.0)
+        nc.scalar.dma_start(out=bias_row[0:1, :], in_=b1[0:1, :])
         warm = keep.tile([P, 1], F32, name="warm")
         warm_out = keep.tile([P, 1], F32, name="warm_out")
         nc.vector.memset(warm[:], 0.0)
         nc.scalar.activation(out=warm_out[:], in_=warm[:], func=ACT.Tanh)
         ident = keep.tile([P, P], F32, name="ident")
         make_identity(nc, ident[:])
+        ones = keep.tile([P, P], BF16, name="ones")
+        nc.vector.memset(ones[:], 1.0)
         count0 = keep.tile([P, 1], F32, name="count0")
         count1 = keep.tile([P, 1], F32, name="count1")
         nc.vector.memset(count0[:], 3.0)
@@ -89,6 +96,12 @@ def tile_predictor_pa_kernel(tc, x, W1, b1, out):
                 in_=xg[g][:, 6:8, 0 : P - 1, :].rearrange("p s r t -> p s (r t)"),
             )
 
+        bias1 = keep.tile([P, C], F32, name="bias1")
+        bias3 = keep.tile([P, C], F32, name="bias3")
+        bias_t0 = keep.tile([P, C], F32, name="bias_t0")
+        bias_t1 = keep.tile([P, C], F32, name="bias_t1")
+        bias_of = {0: bias_t0, 1: bias_t1}
+
         for n in range(TILES // 2):
             j0 = ARRIVAL[2 * n]
             banks = []
@@ -117,7 +130,7 @@ def tile_predictor_pa_kernel(tc, x, W1, b1, out):
 
         def regroup(c):
             wg[c] = stage.tile([P, C, 4], BF16, tag="wg", name="wg%d" % c, align_bytes=64)
-            for copy, c0, c1 in ((nc.vector.tensor_copy, 0, V_COLS), (nc.scalar.copy, V_COLS, C)):
+            for copy, c0, c1 in ((nc.vector.tensor_copy, 0, V_COLS[c]), (nc.scalar.copy, V_COLS[c], C)):
                 copy(
                     out=wg[c][:, c0:c1, :].rearrange("p (c i) t -> p c t i", i=4),
                     in_=w_raw[c][:, :, c0:c1].rearrange("p t (c i) -> p c t i", i=4),
@@ -131,53 +144,60 @@ def tile_predictor_pa_kernel(tc, x, W1, b1, out):
             )
 
         acc = {}
-        for pos, j in enumerate(ARRIVAL):
+        for pos, j in enumerate(EARLY):
             acc[j] = psum.tile([P, C], F32, tag="bank%d" % pos, name="acc%d" % j)
 
-        def mx_pass(j, c):
+        def mx_pass(target, j, c, c0, c1):
             g, tap = divmod(c, TAPS)
             s = slot_of(j, tap)
             nc.tensor.matmul_mx(
-                out=acc[j][:],
+                out=target,
                 lhsT=xc[g][:, s, :].bitcast(FP8X4),
                 lhsT_scale=xs[g][:, s, :],
-                rhs=wc[c][:].bitcast(FP8X4),
-                rhs_scale=ws[c][:],
+                rhs=wc[c][:, c0:c1].bitcast(FP8X4),
+                rhs_scale=ws[c][:, c0:c1],
                 start=(c == 0),
                 stop=(c == CHUNKS - 1),
             )
 
-        regroup(0)
         for c in range(CHUNKS):
             g, tap = divmod(c, TAPS)
-            if c + 1 < CHUNKS:
-                regroup(c + 1)
-            quantise_w(c)
+            regroup(c)
             if g + 1 < SLABS:
                 if tap == 0:
                     shift_copy(g + 1)
                 elif tap == 1:
-                    quantise_x(g + 1, 0, TILES)
-                else:
                     quantise_x(g + 1, TILES, SLOTS)
-            if g + 1 < SLABS:
-                for j in ARRIVAL:
-                    mx_pass(j, c)
-
-        bias3 = keep.tile([P, C], F32, name="bias3")
-        bias_t0 = keep.tile([P, C], F32, name="bias_t0")
-        bias_t1 = keep.tile([P, C], F32, name="bias_t1")
-        nc.scalar.activation(out=bias3[:], in_=bias_raw[:], func=ACT.Copy, scale=3.0)
-        nc.scalar.activation(out=bias_t0[:], in_=bias_raw[:], func=ACT.Copy, scale=count0[:, 0:1])
-        nc.scalar.activation(out=bias_t1[:], in_=bias_raw[:], func=ACT.Copy, scale=count1[:, 0:1])
-        bias_of = {0: bias_t0, 1: bias_t1}
+                else:
+                    quantise_x(g + 1, 0, TILES)
+            quantise_w(c)
+            if c < CM:
+                for j in EARLY:
+                    mx_pass(acc[j][:], j, c, 0, C)
+            if c == 0:
+                bias_ps = psum.tile([P, C], F32, tag="bank7", name="bias_ps")
+                nc.tensor.matmul(out=bias_ps[:], lhsT=ones[:], rhs=bias_row[:], start=True, stop=True)
+            if c == 4:
+                nc.scalar.copy(out=bias1[:], in_=bias_ps[:])
+        nc.vector.tensor_scalar(out=bias3[:], in0=bias1[:], scalar1=3.0, scalar2=None, op0=ALU.mult)
+        nc.vector.tensor_scalar(out=bias_t0[:], in0=bias1[:], scalar1=count0[:, 0:1], scalar2=None, op0=ALU.mult)
+        nc.vector.tensor_scalar(out=bias_t1[:], in0=bias1[:], scalar1=count1[:, 0:1], scalar2=None, op0=ALU.mult)
 
         out_rows = out.rearrange("(i j) c -> i j c", j=TILES)
-        for j in ARRIVAL:
-            for tap in range(TAPS):
-                mx_pass(j, (SLABS - 1) * TAPS + tap)
-            summed = stage.tile([P, C], F32, tag="summed", name="summed%d" % j)
-            nc.vector.tensor_tensor(out=summed[:], in0=acc[j][:], in1=bias_of.get(j, bias3)[:], op=ALU.add)
-            result = stage.tile([P, C], F32, tag="result", name="result%d" % j)
+
+        def finish(sums, j, c0, c1):
+            summed = stage.tile([P, c1 - c0], F32, tag="summed", name="summed%d_%d" % (j, c0))
+            nc.vector.tensor_tensor(out=summed[:], in0=sums, in1=bias_of.get(j, bias3)[:, c0:c1], op=ALU.add)
+            result = stage.tile([P, c1 - c0], F32, tag="result", name="result%d_%d" % (j, c0))
             nc.scalar.activation(out=result[:], in_=summed[:], func=ACT.Tanh)
-            nc.sync.dma_start(out=out_rows[:, j, :], in_=result[:])
+            nc.sync.dma_start(out=out_rows[:, j, c0:c1], in_=result[:])
+
+        for j in EARLY:
+            for c in range(CM, CHUNKS):
+                mx_pass(acc[j][:], j, c, 0, C)
+            finish(acc[j][:], j, 0, C)
+        for bank, c0, c1 in LATE_GROUPS:
+            late = psum.tile([P, c1 - c0], F32, tag="bank%d" % bank, name="late%d" % c0)
+            for c in range(CHUNKS):
+                mx_pass(late[:], LATE, c, c0, c1)
+            finish(late[:], LATE, c0, c1)

@@ -17,14 +17,16 @@ TILES = ROWS // P
 SLABS = E // 512
 CHUNKS = SLABS * TAPS
 SLOTS = TILES + 2
-ARRIVAL = [6, 7, 0, 1, 2, 3, 4, 5]
-EARLY = ARRIVAL[:7]
-LATE = ARRIVAL[7]
-LATE_GROUPS = ((7, 0, 256), (0, 256, 384), (1, 384, 512))
+PAIRS = (6, 0, 2)
+EARLY = (6, 7, 0, 1, 2, 3, 4)
+EARLY_BANK = {6: 2, 7: 3, 0: 4, 1: 7, 2: 5, 3: 6, 4: 0}
+LATE = 5
+LATE_GROUPS = ((1, 0, 256), (2, 256, 384), (3, 384, 512))
 CM = 8
-V_COLS = [336, 256] + [192] * 10
+V_COLS = [336, 400] + [224] * 10
+PRE_WARM = 16
+WARM = True
 FLOPS = 2 * ROWS * E * C * TAPS
-PIN = True
 
 
 def slot_of(j, tap):
@@ -38,24 +40,31 @@ def tile_predictor_pa_kernel(tc, x, W1, b1, out):
         keep = ctx.enter_context(tc.tile_pool(name="keep", bufs=1))
         stage = ctx.enter_context(tc.tile_pool(name="stage", bufs=3))
         psum = ctx.enter_context(tc.psum_pool(name="psum", bufs=1))
-        if PIN:
-            ctx.enter_context(tc.manual_schedule())
+        ctx.enter_context(tc.manual_schedule())
 
         x_rows = x.rearrange("(i j) k -> i j k", j=TILES)
         x_sb = {}
-        for j in ARRIVAL:
-            x_sb[j] = keep.tile([P, E], BF16, name="x_sb%d" % j)
-            nc.sync.dma_start(out=x_sb[j][:], in_=x_rows[:, j, :])
-        w_raw = []
-        for c in range(CHUNKS):
+        w_raw = {}
+
+        def load_w(c):
             g, tap = divmod(c, TAPS)
-            raw = keep.tile([P, 4, C], BF16, name="w_raw%d" % c)
+            w_raw[c] = keep.tile([P, 4, C], BF16, name="w_raw%d" % c)
             nc.sync.dma_start(
-                out=raw[:].rearrange("p (u e) c -> p u (e c)", u=2),
+                out=w_raw[c][:].rearrange("p (u e) c -> p u (e c)", u=2),
                 in_=W1[tap, 512 * g : 512 * (g + 1), :].rearrange("(u q e) c -> q u (e c)", u=2, e=2),
             )
-            w_raw.append(raw)
 
+        load_w(0)
+        for j in (6, 7, 0, 1, 2, 3, 4, 5):
+            x_sb[j] = keep.tile([P, E], BF16, name="x_sb%d" % j)
+            nc.sync.dma_start(out=x_sb[j][:], in_=x_rows[:, j, :])
+        for c in range(1, CHUNKS):
+            load_w(c)
+
+        zeros = keep.tile([P, C], BF16, name="zeros")
+        ones = keep.tile([P, P], BF16, name="ones")
+        nc.vector.memset(zeros[:], 0.0)
+        nc.vector.memset(ones[:], 1.0)
         bias_row = keep.tile([P, C], BF16, name="bias_row")
         nc.vector.memset(bias_row[:], 0.0)
         nc.scalar.dma_start(out=bias_row[0:1, :], in_=b1[0:1, :])
@@ -65,8 +74,6 @@ def tile_predictor_pa_kernel(tc, x, W1, b1, out):
         nc.scalar.activation(out=warm_out[:], in_=warm[:], func=ACT.Tanh)
         ident = keep.tile([P, P], F32, name="ident")
         make_identity(nc, ident[:])
-        ones = keep.tile([P, P], BF16, name="ones")
-        nc.vector.memset(ones[:], 1.0)
         count0 = keep.tile([P, 1], F32, name="count0")
         count1 = keep.tile([P, 1], F32, name="count1")
         nc.vector.memset(count0[:], 3.0)
@@ -82,6 +89,15 @@ def tile_predictor_pa_kernel(tc, x, W1, b1, out):
             xg32.append(grouped[:].bitcast(F32))
             xc.append(keep.tile([P, SLOTS, P], U32, name="xc%d" % g, align_bytes=64))
             xs.append(keep.tile([P, SLOTS, P], U8, name="xs%d" % g, align_bytes=64))
+        bias1 = keep.tile([P, C], F32, name="bias1")
+        bias3 = keep.tile([P, C], F32, name="bias3")
+        bias_t0 = keep.tile([P, C], F32, name="bias_t0")
+        bias_t1 = keep.tile([P, C], F32, name="bias_t1")
+        bias_of = {0: bias_t0, 1: bias_t1}
+        wc, ws, wg = [], [], {}
+        for c in range(CHUNKS):
+            wc.append(keep.tile([P, C], U32, name="wc%d" % c, align_bytes=64))
+            ws.append(keep.tile([P, C], U8, name="ws%d" % c, align_bytes=64))
 
         def quantise_x(g, s0, s1):
             nc.vector.quantize_mx(
@@ -95,38 +111,6 @@ def tile_predictor_pa_kernel(tc, x, W1, b1, out):
                 out=xg[g][:, TILES:SLOTS, 1:P, :].rearrange("p s r t -> p s (r t)"),
                 in_=xg[g][:, 6:8, 0 : P - 1, :].rearrange("p s r t -> p s (r t)"),
             )
-
-        bias1 = keep.tile([P, C], F32, name="bias1")
-        bias3 = keep.tile([P, C], F32, name="bias3")
-        bias_t0 = keep.tile([P, C], F32, name="bias_t0")
-        bias_t1 = keep.tile([P, C], F32, name="bias_t1")
-        bias_of = {0: bias_t0, 1: bias_t1}
-
-        for n in range(TILES // 2):
-            j0 = ARRIVAL[2 * n]
-            banks = []
-            for g in range(SLABS):
-                banks.append(psum.tile([P, 2, 2, P], F32, tag="bank%d" % (4 * (n % 2) + g), name="tp%d_%d" % (n, g)))
-            for jj in range(2):
-                words = x_sb[j0 + jj][:].bitcast(F32)
-                for g in range(SLABS):
-                    for u in range(2):
-                        w0 = 256 * g + 128 * u
-                        nc.tensor.transpose(banks[g][:, jj, u, :], words[:, w0 : w0 + P], ident[:])
-            for g in range(SLABS):
-                copy = nc.scalar.copy if g % 2 == 0 else nc.vector.tensor_copy
-                copy(out=xg32[g][:, j0 : j0 + 2, :, :], in_=banks[g][:].rearrange("p j u r -> p j r u"))
-                if g == 1:
-                    quantise_x(0, j0, j0 + 2)
-            if n == 0:
-                shift_copy(0)
-            if n == 1:
-                quantise_x(0, TILES, SLOTS)
-
-        wc, ws, wg = [], [], {}
-        for c in range(CHUNKS):
-            wc.append(keep.tile([P, C], U32, name="wc%d" % c, align_bytes=64))
-            ws.append(keep.tile([P, C], U8, name="ws%d" % c, align_bytes=64))
 
         def regroup(c):
             wg[c] = stage.tile([P, C, 4], BF16, tag="wg", name="wg%d" % c, align_bytes=64)
@@ -143,9 +127,78 @@ def tile_predictor_pa_kernel(tc, x, W1, b1, out):
                 in_=wg[c][:].rearrange("p c t -> p (c t)"),
             )
 
+        def warm_up(label, times):
+            if WARM:
+                idle = psum.tile([P, C], F32, tag="bank7", name="idle_%s" % label)
+                for k in range(times):
+                    nc.tensor.matmul(out=idle[:], lhsT=ones[:], rhs=zeros[:], start=True, stop=True)
+
+        def transpose_tile(j, targets):
+            words = x_sb[j][:].bitcast(F32)
+            for g in range(SLABS):
+                for u in range(2):
+                    w0 = 256 * g + 128 * u
+                    nc.tensor.transpose(targets[g][:, u, :], words[:, w0 : w0 + P], ident[:])
+
+        warm_up("start", PRE_WARM)
+        regroup(0)
+        quantise_w(0)
+
+        fill = 0
+        for n, j0 in enumerate(PAIRS):
+            banks = []
+            for g in range(SLABS):
+                banks.append(psum.tile([P, 2, 2, P], F32, tag="bank%d" % (fill % 7), name="tp%d_%d" % (n, g)))
+                fill += 1
+            transpose_tile(j0, [b[:, 0, :, :] for b in banks])
+            if n == 0:
+                bias_ps = psum.tile([P, C], F32, tag="bank7", name="bias_ps")
+                nc.tensor.matmul(out=bias_ps[:], lhsT=ones[:], rhs=bias_row[:], start=True, stop=True)
+                nc.scalar.copy(out=bias1[:], in_=bias_ps[:])
+            else:
+                warm_up("a%d" % n, 1)
+            transpose_tile(j0 + 1, [b[:, 1, :, :] for b in banks])
+            warm_up("b%d" % n, 1)
+
+            def evacuate(copy, g):
+                copy(out=xg32[g][:, j0 : j0 + 2, :, :], in_=banks[g][:].rearrange("p j u r -> p j r u"))
+
+            evacuate(nc.scalar.copy, 0)
+            evacuate(nc.vector.tensor_copy, 1)
+            evacuate(nc.scalar.copy, 2)
+            quantise_x(0, j0, j0 + 2)
+            evacuate(nc.scalar.copy, 3)
+            if n == 0:
+                shift_copy(0)
+            if n == 1:
+                quantise_x(0, TILES, SLOTS)
+            for g in range(1, SLABS):
+                quantise_x(g, j0, j0 + 2)
+
+        single = {}
+        for j in (4, 5):
+            single[j] = []
+            for h in range(2):
+                single[j].append(psum.tile([P, 2, 2, P], F32, tag="bank%d" % (fill % 7), name="ts%d_%d" % (j, h)))
+                fill += 1
+
+        def evacuate_single(copy, j, g):
+            copy(out=xg32[g][:, j, :, :], in_=single[j][g // 2][:, g % 2, :, :].rearrange("p u r -> p r u"))
+
+        transpose_tile(4, [single[4][g // 2][:, g % 2, :, :] for g in range(SLABS)])
+        warm_up("c", 1)
+        evacuate_single(nc.scalar.copy, 4, 0)
+        evacuate_single(nc.vector.tensor_copy, 4, 1)
+        evacuate_single(nc.scalar.copy, 4, 2)
+        evacuate_single(nc.vector.tensor_copy, 4, 3)
+        quantise_x(0, 4, 5)
+        transpose_tile(5, [single[5][g // 2][:, g % 2, :, :] for g in range(SLABS)])
+        evacuate_single(nc.scalar.copy, 5, 0)
+        evacuate_single(nc.vector.tensor_copy, 5, 1)
+
         acc = {}
-        for pos, j in enumerate(EARLY):
-            acc[j] = psum.tile([P, C], F32, tag="bank%d" % pos, name="acc%d" % j)
+        for j in EARLY:
+            acc[j] = psum.tile([P, C], F32, tag="bank%d" % EARLY_BANK[j], name="acc%d" % j)
 
         def mx_pass(target, j, c, c0, c1):
             g, tap = divmod(c, TAPS)
@@ -160,25 +213,28 @@ def tile_predictor_pa_kernel(tc, x, W1, b1, out):
                 stop=(c == CHUNKS - 1),
             )
 
-        for c in range(CHUNKS):
-            g, tap = divmod(c, TAPS)
+        for j in EARLY:
+            mx_pass(acc[j][:], j, 0, 0, C)
+        regroup(1)
+        quantise_w(1)
+        quantise_x(0, 5, 6)
+        for j in (7, 0, 1, 2, 3, 4, 6):
+            mx_pass(acc[j][:], j, 1, 0, C)
+        evacuate_single(nc.scalar.copy, 5, 2)
+        evacuate_single(nc.vector.tensor_copy, 5, 3)
+        for c in range(2, CHUNKS):
             regroup(c)
-            if g + 1 < SLABS:
-                if tap == 0:
-                    shift_copy(g + 1)
-                elif tap == 1:
-                    quantise_x(g + 1, TILES, SLOTS)
+            g_next = c // 2
+            if g_next < SLABS:
+                if c % 2 == 0:
+                    quantise_x(g_next, 4, 6)
+                    shift_copy(g_next)
                 else:
-                    quantise_x(g + 1, 0, TILES)
+                    quantise_x(g_next, TILES, SLOTS)
             quantise_w(c)
             if c < CM:
                 for j in EARLY:
                     mx_pass(acc[j][:], j, c, 0, C)
-            if c == 0:
-                bias_ps = psum.tile([P, C], F32, tag="bank7", name="bias_ps")
-                nc.tensor.matmul(out=bias_ps[:], lhsT=ones[:], rhs=bias_row[:], start=True, stop=True)
-            if c == 4:
-                nc.scalar.copy(out=bias1[:], in_=bias_ps[:])
         nc.vector.tensor_scalar(out=bias3[:], in0=bias1[:], scalar1=3.0, scalar2=None, op0=ALU.mult)
         nc.vector.tensor_scalar(out=bias_t0[:], in0=bias1[:], scalar1=count0[:, 0:1], scalar2=None, op0=ALU.mult)
         nc.vector.tensor_scalar(out=bias_t1[:], in0=bias1[:], scalar1=count1[:, 0:1], scalar2=None, op0=ALU.mult)

@@ -22,7 +22,7 @@ EARLY = (6, 7, 0, 1, 2, 3, 4)
 EARLY_BANK = {6: 2, 7: 3, 0: 4, 1: 7, 2: 5, 3: 6, 4: 0}
 LATE = 5
 LATE_GROUPS = ((1, 0, 256), (2, 256, 384), (3, 384, 512))
-CM = 8
+CM = 9
 V_COLS = [336, 400] + [224] * 10
 PRE_WARM = 16
 WARM = True

@@ -244,7 +244,7 @@ def tile_predictor_pa_kernel(tc, x, W1, b1, out):
         def finish(sums, j, c0, c1):
             summed = stage.tile([P, c1 - c0], F32, tag="summed", name="summed%d_%d" % (j, c0))
             nc.vector.tensor_tensor(out=summed[:], in0=sums, in1=bias_of.get(j, bias3)[:, c0:c1], op=ALU.add)
-            result = stage.tile([P, c1 - c0], F32, tag="result", name="result%d_%d" % (j, c0))
+            result = keep.tile([P, c1 - c0], F32, name="result%d_%d" % (j, c0))
             nc.scalar.activation(out=result[:], in_=summed[:], func=ACT.Tanh)
             nc.sync.dma_start(out=out_rows[:, j, c0:c1], in_=result[:])
 

@@ -25,7 +25,7 @@ LATE_GROUPS = ((1, 0, 256), (2, 256, 384), (3, 384, 512))
 CM = 9
 V_COLS = [336, 400] + [224] * 10
 PRE_WARM = 16
-WARM = True
+WARM = False
 FLOPS = 2 * ROWS * E * C * TAPS
 
 

@@ -12,26 +12,28 @@ ACT = mybir.ActivationFunctionType
 ALU = mybir.AluOpType
 
 P = 128
-ROWS, E, C, TAPS = 1024, 2048, 512, 3
-TILES = ROWS // P
-SLABS = E // 512
+ROWS, K_DIM, COLS, TAPS = 1024, 2048, 512, 3
+SLAB = 4 * P
+SLABS = K_DIM // SLAB
 CHUNKS = SLABS * TAPS
+TILES = ROWS // P
 SLOTS = TILES + 2
+MOVED = 6
+
 PAIRS = (6, 0, 2)
+SINGLES = (4, 5)
 EARLY = (6, 7, 0, 1, 2, 3, 4)
-EARLY_BANK = {6: 2, 7: 3, 0: 4, 1: 7, 2: 5, 3: 6, 4: 0}
 LATE = 5
-LATE_GROUPS = ((1, 0, 256), (2, 256, 384), (3, 384, 512))
-CM = 9
-V_COLS = [336, 400] + [224] * 10
-PRE_WARM = 16
-WARM = False
-FLOPS = 2 * ROWS * E * C * TAPS
+LATE_GROUPS = ((7, 0, 256), (0, 256, 384), (1, 384, 512))
+CHUNK_BY_CHUNK = 9
+VECTOR_COLS = (336, 400, 224) + (192,) * 9
+
+FLOPS = 2 * ROWS * K_DIM * COLS * TAPS
 
 
 def slot_of(j, tap):
-    src = j - tap
-    return src if src >= 0 else src + SLOTS
+    source = j - tap
+    return source if source >= 0 else source + SLOTS
 
 
 def tile_predictor_pa_kernel(tc, x, W1, b1, out):
@@ -46,32 +48,30 @@ def tile_predictor_pa_kernel(tc, x, W1, b1, out):
         x_sb = {}
         w_raw = {}
 
-        def load_w(c):
+        def load_chunk(c):
             g, tap = divmod(c, TAPS)
-            w_raw[c] = keep.tile([P, 4, C], BF16, name="w_raw%d" % c)
+            w_raw[c] = keep.tile([P, 4, COLS], BF16, name="w_raw%d" % c)
             nc.sync.dma_start(
                 out=w_raw[c][:].rearrange("p (u e) c -> p u (e c)", u=2),
-                in_=W1[tap, 512 * g : 512 * (g + 1), :].rearrange("(u q e) c -> q u (e c)", u=2, e=2),
+                in_=W1[tap, SLAB * g : SLAB * (g + 1), :].rearrange("(u q e) c -> q u (e c)", u=2, e=2),
             )
 
-        load_w(0)
+        load_chunk(0)
         for j in (6, 7, 0, 1, 2, 3, 4, 5):
-            x_sb[j] = keep.tile([P, E], BF16, name="x_sb%d" % j)
+            x_sb[j] = keep.tile([P, K_DIM], BF16, name="x_sb%d" % j)
             nc.sync.dma_start(out=x_sb[j][:], in_=x_rows[:, j, :])
         for c in range(1, CHUNKS):
-            load_w(c)
+            load_chunk(c)
 
-        zeros = keep.tile([P, C], BF16, name="zeros")
-        ones = keep.tile([P, P], BF16, name="ones")
-        nc.vector.memset(zeros[:], 0.0)
-        nc.vector.memset(ones[:], 1.0)
-        bias_row = keep.tile([P, C], BF16, name="bias_row")
+        bias_row = keep.tile([P, COLS], BF16, name="bias_row")
         nc.vector.memset(bias_row[:], 0.0)
         nc.scalar.dma_start(out=bias_row[0:1, :], in_=b1[0:1, :])
-        warm = keep.tile([P, 1], F32, name="warm")
-        warm_out = keep.tile([P, 1], F32, name="warm_out")
-        nc.vector.memset(warm[:], 0.0)
-        nc.scalar.activation(out=warm_out[:], in_=warm[:], func=ACT.Tanh)
+        ones = keep.tile([P, P], BF16, name="ones")
+        nc.vector.memset(ones[:], 1.0)
+        table_in = keep.tile([P, 1], F32, name="table_in")
+        table_out = keep.tile([P, 1], F32, name="table_out")
+        nc.vector.memset(table_in[:], 0.0)
+        nc.scalar.activation(out=table_out[:], in_=table_in[:], func=ACT.Tanh)
         ident = keep.tile([P, P], F32, name="ident")
         make_identity(nc, ident[:])
         count0 = keep.tile([P, 1], F32, name="count0")
@@ -81,179 +81,173 @@ def tile_predictor_pa_kernel(tc, x, W1, b1, out):
         nc.vector.memset(count1[:], 3.0)
         nc.vector.memset(count1[0:1, :], 2.0)
 
-        xg, xg32, xc, xs = [], [], [], []
+        xg, xg_words, xc, xs = [], [], [], []
         for g in range(SLABS):
             grouped = keep.tile([P, SLOTS, P, 4], BF16, name="xg%d" % g, align_bytes=64)
             nc.vector.memset(grouped[:, TILES:SLOTS, :, :], 0.0)
             xg.append(grouped)
-            xg32.append(grouped[:].bitcast(F32))
+            xg_words.append(grouped[:].bitcast(F32))
             xc.append(keep.tile([P, SLOTS, P], U32, name="xc%d" % g, align_bytes=64))
             xs.append(keep.tile([P, SLOTS, P], U8, name="xs%d" % g, align_bytes=64))
-        bias1 = keep.tile([P, C], F32, name="bias1")
-        bias3 = keep.tile([P, C], F32, name="bias3")
-        bias_t0 = keep.tile([P, C], F32, name="bias_t0")
-        bias_t1 = keep.tile([P, C], F32, name="bias_t1")
-        bias_of = {0: bias_t0, 1: bias_t1}
         wc, ws, wg = [], [], {}
         for c in range(CHUNKS):
-            wc.append(keep.tile([P, C], U32, name="wc%d" % c, align_bytes=64))
-            ws.append(keep.tile([P, C], U8, name="ws%d" % c, align_bytes=64))
+            wc.append(keep.tile([P, COLS], U32, name="wc%d" % c, align_bytes=64))
+            ws.append(keep.tile([P, COLS], U8, name="ws%d" % c, align_bytes=64))
+        bias1 = keep.tile([P, COLS], F32, name="bias1")
+        bias3 = keep.tile([P, COLS], F32, name="bias3")
+        bias_tile0 = keep.tile([P, COLS], F32, name="bias_tile0")
+        bias_tile1 = keep.tile([P, COLS], F32, name="bias_tile1")
+        bias_of = {0: bias_tile0, 1: bias_tile1}
 
-        def quantise_x(g, s0, s1):
+        def quantise_x(g, first, end):
             nc.vector.quantize_mx(
-                out=xc[g][:, s0:s1, :].rearrange("p s r -> p (s r)").bitcast(FP8X4),
-                scales=xs[g][:, s0:s1, :].rearrange("p s r -> p (s r)"),
-                in_=xg[g][:, s0:s1, :, :].rearrange("p s r t -> p (s r t)"),
+                out=xc[g][:, first:end, :].rearrange("p s r -> p (s r)").bitcast(FP8X4),
+                scales=xs[g][:, first:end, :].rearrange("p s r -> p (s r)"),
+                in_=xg[g][:, first:end, :, :].rearrange("p s r t -> p (s r t)"),
             )
 
-        def shift_copy(g):
+        def move_by_one_column(g):
             nc.vector.tensor_copy(
                 out=xg[g][:, TILES:SLOTS, 1:P, :].rearrange("p s r t -> p s (r t)"),
-                in_=xg[g][:, 6:8, 0 : P - 1, :].rearrange("p s r t -> p s (r t)"),
+                in_=xg[g][:, MOVED : MOVED + 2, 0 : P - 1, :].rearrange("p s r t -> p s (r t)"),
             )
 
         def regroup(c):
-            wg[c] = stage.tile([P, C, 4], BF16, tag="wg", name="wg%d" % c, align_bytes=64)
-            for copy, c0, c1 in ((nc.vector.tensor_copy, 0, V_COLS[c]), (nc.scalar.copy, V_COLS[c], C)):
+            wg[c] = stage.tile([P, COLS, 4], BF16, tag="wg", name="wg%d" % c, align_bytes=64)
+            for copy, first, end in (
+                (nc.vector.tensor_copy, 0, VECTOR_COLS[c]),
+                (nc.scalar.copy, VECTOR_COLS[c], COLS),
+            ):
                 copy(
-                    out=wg[c][:, c0:c1, :].rearrange("p (c i) t -> p c t i", i=4),
-                    in_=w_raw[c][:, :, c0:c1].rearrange("p t (c i) -> p c t i", i=4),
+                    out=wg[c][:, first:end, :].rearrange("p (c i) t -> p c t i", i=4),
+                    in_=w_raw[c][:, :, first:end].rearrange("p t (c i) -> p c t i", i=4),
                 )
 
-        def quantise_w(c):
+        def quantise_chunk(c):
             nc.vector.quantize_mx(
                 out=wc[c][:].bitcast(FP8X4),
                 scales=ws[c][:],
                 in_=wg[c][:].rearrange("p c t -> p (c t)"),
             )
 
-        def warm_up(label, times):
-            if WARM:
-                idle = psum.tile([P, C], F32, tag="bank7", name="idle_%s" % label)
-                for k in range(times):
-                    nc.tensor.matmul(out=idle[:], lhsT=ones[:], rhs=zeros[:], start=True, stop=True)
-
         def transpose_tile(j, targets):
             words = x_sb[j][:].bitcast(F32)
             for g in range(SLABS):
                 for u in range(2):
-                    w0 = 256 * g + 128 * u
-                    nc.tensor.transpose(targets[g][:, u, :], words[:, w0 : w0 + P], ident[:])
+                    first = 256 * g + P * u
+                    nc.tensor.transpose(targets[g][:, u, :], words[:, first : first + P], ident[:])
 
-        warm_up("start", PRE_WARM)
         regroup(0)
-        quantise_w(0)
+        quantise_chunk(0)
 
-        fill = 0
         for n, j0 in enumerate(PAIRS):
             banks = []
             for g in range(SLABS):
-                banks.append(psum.tile([P, 2, 2, P], F32, tag="bank%d" % (fill % 7), name="tp%d_%d" % (n, g)))
-                fill += 1
-            transpose_tile(j0, [b[:, 0, :, :] for b in banks])
+                banks.append(psum.tile([P, 2, 2, P], F32, tag="bank%d" % (4 * (n % 2) + g), name="pair%d_%d" % (j0, g)))
+            transpose_tile(j0, [bank[:, 0, :, :] for bank in banks])
             if n == 0:
-                bias_ps = psum.tile([P, C], F32, tag="bank7", name="bias_ps")
+                bias_ps = psum.tile([P, COLS], F32, tag="bank7", name="bias_ps")
                 nc.tensor.matmul(out=bias_ps[:], lhsT=ones[:], rhs=bias_row[:], start=True, stop=True)
                 nc.scalar.copy(out=bias1[:], in_=bias_ps[:])
-            else:
-                warm_up("a%d" % n, 1)
-            transpose_tile(j0 + 1, [b[:, 1, :, :] for b in banks])
-            warm_up("b%d" % n, 1)
+            transpose_tile(j0 + 1, [bank[:, 1, :, :] for bank in banks])
 
-            def evacuate(copy, g):
-                copy(out=xg32[g][:, j0 : j0 + 2, :, :], in_=banks[g][:].rearrange("p j u r -> p j r u"))
+            def copy_out_pair(copy, g):
+                copy(out=xg_words[g][:, j0 : j0 + 2, :, :], in_=banks[g][:].rearrange("p j u r -> p j r u"))
 
-            evacuate(nc.scalar.copy, 0)
-            evacuate(nc.vector.tensor_copy, 1)
-            evacuate(nc.scalar.copy, 2)
+            copy_out_pair(nc.scalar.copy, 0)
+            copy_out_pair(nc.vector.tensor_copy, 1)
+            copy_out_pair(nc.scalar.copy, 2)
             quantise_x(0, j0, j0 + 2)
-            evacuate(nc.scalar.copy, 3)
+            copy_out_pair(nc.scalar.copy, 3)
             if n == 0:
-                shift_copy(0)
+                move_by_one_column(0)
             if n == 1:
                 quantise_x(0, TILES, SLOTS)
-            for g in range(1, SLABS):
+            for g in range(1, SLABS if n < 2 else 2):
                 quantise_x(g, j0, j0 + 2)
 
-        single = {}
-        for j in (4, 5):
-            single[j] = []
+        halves = {}
+        for n, j in enumerate(SINGLES):
+            halves[j] = []
             for h in range(2):
-                single[j].append(psum.tile([P, 2, 2, P], F32, tag="bank%d" % (fill % 7), name="ts%d_%d" % (j, h)))
-                fill += 1
+                halves[j].append(psum.tile([P, 2, 2, P], F32, tag="bank%d" % (4 + 2 * n + h), name="single%d_%d" % (j, h)))
 
-        def evacuate_single(copy, j, g):
-            copy(out=xg32[g][:, j, :, :], in_=single[j][g // 2][:, g % 2, :, :].rearrange("p u r -> p r u"))
+        def copy_out_single(copy, j, g):
+            copy(out=xg_words[g][:, j, :, :], in_=halves[j][g // 2][:, g % 2, :, :].rearrange("p u r -> p r u"))
 
-        transpose_tile(4, [single[4][g // 2][:, g % 2, :, :] for g in range(SLABS)])
-        warm_up("c", 1)
-        evacuate_single(nc.scalar.copy, 4, 0)
-        evacuate_single(nc.vector.tensor_copy, 4, 1)
-        evacuate_single(nc.scalar.copy, 4, 2)
-        evacuate_single(nc.vector.tensor_copy, 4, 3)
+        transpose_tile(4, [halves[4][g // 2][:, g % 2, :, :] for g in range(SLABS)])
+        copy_out_single(nc.scalar.copy, 4, 0)
+        copy_out_single(nc.vector.tensor_copy, 4, 1)
+        copy_out_single(nc.scalar.copy, 4, 2)
+        copy_out_single(nc.vector.tensor_copy, 4, 3)
         quantise_x(0, 4, 5)
-        transpose_tile(5, [single[5][g // 2][:, g % 2, :, :] for g in range(SLABS)])
-        evacuate_single(nc.scalar.copy, 5, 0)
-        evacuate_single(nc.vector.tensor_copy, 5, 1)
+        transpose_tile(5, [halves[5][g // 2][:, g % 2, :, :] for g in range(SLABS)])
+        copy_out_single(nc.scalar.copy, 5, 0)
+        copy_out_single(nc.vector.tensor_copy, 5, 1)
 
         acc = {}
-        for j in EARLY:
-            acc[j] = psum.tile([P, C], F32, tag="bank%d" % EARLY_BANK[j], name="acc%d" % j)
+        for bank, j in enumerate(EARLY):
+            acc[j] = psum.tile([P, COLS], F32, tag="bank%d" % bank, name="acc%d" % j)
 
-        def mx_pass(target, j, c, c0, c1):
+        def mx_pass(target, j, c, first, end):
             g, tap = divmod(c, TAPS)
             s = slot_of(j, tap)
             nc.tensor.matmul_mx(
                 out=target,
                 lhsT=xc[g][:, s, :].bitcast(FP8X4),
                 lhsT_scale=xs[g][:, s, :],
-                rhs=wc[c][:, c0:c1].bitcast(FP8X4),
-                rhs_scale=ws[c][:, c0:c1],
+                rhs=wc[c][:, first:end].bitcast(FP8X4),
+                rhs_scale=ws[c][:, first:end],
                 start=(c == 0),
                 stop=(c == CHUNKS - 1),
             )
 
         for j in EARLY:
-            mx_pass(acc[j][:], j, 0, 0, C)
+            mx_pass(acc[j][:], j, 0, 0, COLS)
         regroup(1)
-        quantise_w(1)
+        quantise_chunk(1)
         quantise_x(0, 5, 6)
         for j in (7, 0, 1, 2, 3, 4, 6):
-            mx_pass(acc[j][:], j, 1, 0, C)
-        evacuate_single(nc.scalar.copy, 5, 2)
-        evacuate_single(nc.vector.tensor_copy, 5, 3)
+            mx_pass(acc[j][:], j, 1, 0, COLS)
+        copy_out_single(nc.scalar.copy, 5, 2)
+        copy_out_single(nc.vector.tensor_copy, 5, 3)
         for c in range(2, CHUNKS):
             regroup(c)
-            g_next = c // 2
-            if g_next < SLABS:
+            g = c // 2
+            if g < SLABS:
                 if c % 2 == 0:
-                    quantise_x(g_next, 4, 6)
-                    shift_copy(g_next)
+                    quantise_x(g, 4, 6)
                 else:
-                    quantise_x(g_next, TILES, SLOTS)
-            quantise_w(c)
-            if c < CM:
+                    move_by_one_column(g)
+            quantise_chunk(c)
+            if g < SLABS:
+                if c % 2 == 1:
+                    quantise_x(g, TILES, SLOTS)
+                elif g >= 2:
+                    quantise_x(g, 2, 4)
+            if c < CHUNK_BY_CHUNK:
                 for j in EARLY:
-                    mx_pass(acc[j][:], j, c, 0, C)
+                    mx_pass(acc[j][:], j, c, 0, COLS)
+
         nc.vector.tensor_scalar(out=bias3[:], in0=bias1[:], scalar1=3.0, scalar2=None, op0=ALU.mult)
-        nc.vector.tensor_scalar(out=bias_t0[:], in0=bias1[:], scalar1=count0[:, 0:1], scalar2=None, op0=ALU.mult)
-        nc.vector.tensor_scalar(out=bias_t1[:], in0=bias1[:], scalar1=count1[:, 0:1], scalar2=None, op0=ALU.mult)
+        nc.vector.tensor_scalar(out=bias_tile0[:], in0=bias1[:], scalar1=count0[:, 0:1], scalar2=None, op0=ALU.mult)
+        nc.vector.tensor_scalar(out=bias_tile1[:], in0=bias1[:], scalar1=count1[:, 0:1], scalar2=None, op0=ALU.mult)
 
         out_rows = out.rearrange("(i j) c -> i j c", j=TILES)
 
-        def finish(sums, j, c0, c1):
-            summed = stage.tile([P, c1 - c0], F32, tag="summed", name="summed%d_%d" % (j, c0))
-            nc.vector.tensor_tensor(out=summed[:], in0=sums, in1=bias_of.get(j, bias3)[:, c0:c1], op=ALU.add)
-            result = keep.tile([P, c1 - c0], F32, name="result%d_%d" % (j, c0))
+        def finish(sums, j, first, end):
+            summed = stage.tile([P, end - first], F32, tag="summed", name="summed%d_%d" % (j, first))
+            nc.vector.tensor_tensor(out=summed[:], in0=sums, in1=bias_of.get(j, bias3)[:, first:end], op=ALU.add)
+            result = keep.tile([P, end - first], F32, name="result%d_%d" % (j, first))
             nc.scalar.activation(out=result[:], in_=summed[:], func=ACT.Tanh)
-            nc.sync.dma_start(out=out_rows[:, j, c0:c1], in_=result[:])
+            nc.sync.dma_start(out=out_rows[:, j, first:end], in_=result[:])
 
         for j in EARLY:
-            for c in range(CM, CHUNKS):
-                mx_pass(acc[j][:], j, c, 0, C)
-            finish(acc[j][:], j, 0, C)
-        for bank, c0, c1 in LATE_GROUPS:
-            late = psum.tile([P, c1 - c0], F32, tag="bank%d" % bank, name="late%d" % c0)
+            for c in range(CHUNK_BY_CHUNK, CHUNKS):
+                mx_pass(acc[j][:], j, c, 0, COLS)
+            finish(acc[j][:], j, 0, COLS)
+        for bank, first, end in LATE_GROUPS:
+            late = psum.tile([P, end - first], F32, tag="bank%d" % bank, name="late%d" % first)
             for c in range(CHUNKS):
-                mx_pass(late[:], LATE, c, c0, c1)
-            finish(late[:], LATE, c0, c1)
+                mx_pass(late[:], LATE, c, first, end)
+            finish(late[:], LATE, first, end)

@@ -42,7 +42,6 @@ def tile_predictor_pa_kernel(tc, x, W1, b1, out):
         keep = ctx.enter_context(tc.tile_pool(name="keep", bufs=1))
         stage = ctx.enter_context(tc.tile_pool(name="stage", bufs=3))
         psum = ctx.enter_context(tc.psum_pool(name="psum", bufs=1))
-        ctx.enter_context(tc.manual_schedule())
 
         x_rows = x.rearrange("(i j) k -> i j k", j=TILES)
         x_sb = {}

from contextlib import ExitStack

import concourse.mybir as mybir
from concourse.masks import make_identity

F32 = mybir.dt.float32
BF16 = mybir.dt.bfloat16
U32 = mybir.dt.uint32
U8 = mybir.dt.uint8
FP8X4 = mybir.dt.float8_e4m3fn_x4
ACT = mybir.ActivationFunctionType
ALU = mybir.AluOpType

P = 128
ROWS, K_DIM, COLS, TAPS = 1024, 2048, 512, 3
SLAB = 4 * P
SLABS = K_DIM // SLAB
CHUNKS = SLABS * TAPS
TILES = ROWS // P
SLOTS = TILES + 2
MOVED = 6

PAIRS = (6, 0, 2)
SINGLES = (4, 5)
EARLY = (6, 7, 0, 1, 2, 3, 4)
LATE = 5
LATE_GROUPS = ((7, 0, 256), (0, 256, 384), (1, 384, 512))
CHUNK_BY_CHUNK = 9
VECTOR_COLS = (336, 400, 224) + (192,) * 9

FLOPS = 2 * ROWS * K_DIM * COLS * TAPS


def slot_of(j, tap):
    source = j - tap
    return source if source >= 0 else source + SLOTS


def tile_predictor_pa_kernel(tc, x, W1, b1, out):
    nc = tc.nc
    with ExitStack() as ctx:
        keep = ctx.enter_context(tc.tile_pool(name="keep", bufs=1))
        stage = ctx.enter_context(tc.tile_pool(name="stage", bufs=3))
        psum = ctx.enter_context(tc.psum_pool(name="psum", bufs=1))

        x_rows = x.rearrange("(i j) k -> i j k", j=TILES)
        x_sb = {}
        w_raw = {}

        def load_chunk(c):
            g, tap = divmod(c, TAPS)
            w_raw[c] = keep.tile([P, 4, COLS], BF16, name="w_raw%d" % c)
            nc.sync.dma_start(
                out=w_raw[c][:].rearrange("p (u e) c -> p u (e c)", u=2),
                in_=W1[tap, SLAB * g : SLAB * (g + 1), :].rearrange("(u q e) c -> q u (e c)", u=2, e=2),
            )

        load_chunk(0)
        for j in (6, 7, 0, 1, 2, 3, 4, 5):
            x_sb[j] = keep.tile([P, K_DIM], BF16, name="x_sb%d" % j)
            nc.sync.dma_start(out=x_sb[j][:], in_=x_rows[:, j, :])
        for c in range(1, CHUNKS):
            load_chunk(c)

        bias_row = keep.tile([P, COLS], BF16, name="bias_row")
        nc.vector.memset(bias_row[:], 0.0)
        nc.scalar.dma_start(out=bias_row[0:1, :], in_=b1[0:1, :])
        ones = keep.tile([P, P], BF16, name="ones")
        nc.vector.memset(ones[:], 1.0)
        table_in = keep.tile([P, 1], F32, name="table_in")
        table_out = keep.tile([P, 1], F32, name="table_out")
        nc.vector.memset(table_in[:], 0.0)
        nc.scalar.activation(out=table_out[:], in_=table_in[:], func=ACT.Tanh)
        ident = keep.tile([P, P], F32, name="ident")
        make_identity(nc, ident[:])
        count0 = keep.tile([P, 1], F32, name="count0")
        count1 = keep.tile([P, 1], F32, name="count1")
        nc.vector.memset(count0[:], 3.0)
        nc.vector.memset(count0[0:1, :], 1.0)
        nc.vector.memset(count1[:], 3.0)
        nc.vector.memset(count1[0:1, :], 2.0)

        xg, xg_words, xc, xs = [], [], [], []
        for g in range(SLABS):
            grouped = keep.tile([P, SLOTS, P, 4], BF16, name="xg%d" % g, align_bytes=64)
            nc.vector.memset(grouped[:, TILES:SLOTS, :, :], 0.0)
            xg.append(grouped)
            xg_words.append(grouped[:].bitcast(F32))
            xc.append(keep.tile([P, SLOTS, P], U32, name="xc%d" % g, align_bytes=64))
            xs.append(keep.tile([P, SLOTS, P], U8, name="xs%d" % g, align_bytes=64))
        wc, ws, wg = [], [], {}
        for c in range(CHUNKS):
            wc.append(keep.tile([P, COLS], U32, name="wc%d" % c, align_bytes=64))
            ws.append(keep.tile([P, COLS], U8, name="ws%d" % c, align_bytes=64))
        bias1 = keep.tile([P, COLS], F32, name="bias1")
        bias3 = keep.tile([P, COLS], F32, name="bias3")
        bias_tile0 = keep.tile([P, COLS], F32, name="bias_tile0")
        bias_tile1 = keep.tile([P, COLS], F32, name="bias_tile1")
        bias_of = {0: bias_tile0, 1: bias_tile1}

        def quantise_x(g, first, end):
            nc.vector.quantize_mx(
                out=xc[g][:, first:end, :].rearrange("p s r -> p (s r)").bitcast(FP8X4),
                scales=xs[g][:, first:end, :].rearrange("p s r -> p (s r)"),
                in_=xg[g][:, first:end, :, :].rearrange("p s r t -> p (s r t)"),
            )

        def move_by_one_column(g):
            nc.vector.tensor_copy(
                out=xg[g][:, TILES:SLOTS, 1:P, :].rearrange("p s r t -> p s (r t)"),
                in_=xg[g][:, MOVED : MOVED + 2, 0 : P - 1, :].rearrange("p s r t -> p s (r t)"),
            )

        def regroup(c):
            wg[c] = stage.tile([P, COLS, 4], BF16, tag="wg", name="wg%d" % c, align_bytes=64)
            for copy, first, end in (
                (nc.vector.tensor_copy, 0, VECTOR_COLS[c]),
                (nc.scalar.copy, VECTOR_COLS[c], COLS),
            ):
                copy(
                    out=wg[c][:, first:end, :].rearrange("p (c i) t -> p c t i", i=4),
                    in_=w_raw[c][:, :, first:end].rearrange("p t (c i) -> p c t i", i=4),
                )

        def quantise_chunk(c):
            nc.vector.quantize_mx(
                out=wc[c][:].bitcast(FP8X4),
                scales=ws[c][:],
                in_=wg[c][:].rearrange("p c t -> p (c t)"),
            )

        def transpose_tile(j, targets):
            words = x_sb[j][:].bitcast(F32)
            for g in range(SLABS):
                for u in range(2):
                    first = 256 * g + P * u
                    nc.tensor.transpose(targets[g][:, u, :], words[:, first : first + P], ident[:])

        regroup(0)
        quantise_chunk(0)

        for n, j0 in enumerate(PAIRS):
            banks = []
            for g in range(SLABS):
                banks.append(psum.tile([P, 2, 2, P], F32, tag="bank%d" % (4 * (n % 2) + g), name="pair%d_%d" % (j0, g)))
            transpose_tile(j0, [bank[:, 0, :, :] for bank in banks])
            if n == 0:
                bias_ps = psum.tile([P, COLS], F32, tag="bank7", name="bias_ps")
                nc.tensor.matmul(out=bias_ps[:], lhsT=ones[:], rhs=bias_row[:], start=True, stop=True)
                nc.scalar.copy(out=bias1[:], in_=bias_ps[:])
            transpose_tile(j0 + 1, [bank[:, 1, :, :] for bank in banks])

            def copy_out_pair(copy, g):
                copy(out=xg_words[g][:, j0 : j0 + 2, :, :], in_=banks[g][:].rearrange("p j u r -> p j r u"))

            copy_out_pair(nc.scalar.copy, 0)
            copy_out_pair(nc.vector.tensor_copy, 1)
            copy_out_pair(nc.scalar.copy, 2)
            quantise_x(0, j0, j0 + 2)
            copy_out_pair(nc.scalar.copy, 3)
            if n == 0:
                move_by_one_column(0)
            if n == 1:
                quantise_x(0, TILES, SLOTS)
            for g in range(1, SLABS if n < 2 else 2):
                quantise_x(g, j0, j0 + 2)

        halves = {}
        for n, j in enumerate(SINGLES):
            halves[j] = []
            for h in range(2):
                halves[j].append(psum.tile([P, 2, 2, P], F32, tag="bank%d" % (4 + 2 * n + h), name="single%d_%d" % (j, h)))

        def copy_out_single(copy, j, g):
            copy(out=xg_words[g][:, j, :, :], in_=halves[j][g // 2][:, g % 2, :, :].rearrange("p u r -> p r u"))

        transpose_tile(4, [halves[4][g // 2][:, g % 2, :, :] for g in range(SLABS)])
        copy_out_single(nc.scalar.copy, 4, 0)
        copy_out_single(nc.vector.tensor_copy, 4, 1)
        copy_out_single(nc.scalar.copy, 4, 2)
        copy_out_single(nc.vector.tensor_copy, 4, 3)
        quantise_x(0, 4, 5)
        transpose_tile(5, [halves[5][g // 2][:, g % 2, :, :] for g in range(SLABS)])
        copy_out_single(nc.scalar.copy, 5, 0)
        copy_out_single(nc.vector.tensor_copy, 5, 1)

        acc = {}
        for bank, j in enumerate(EARLY):
            acc[j] = psum.tile([P, COLS], F32, tag="bank%d" % bank, name="acc%d" % j)

        def mx_pass(target, j, c, first, end):
            g, tap = divmod(c, TAPS)
            s = slot_of(j, tap)
            nc.tensor.matmul_mx(
                out=target,
                lhsT=xc[g][:, s, :].bitcast(FP8X4),
                lhsT_scale=xs[g][:, s, :],
                rhs=wc[c][:, first:end].bitcast(FP8X4),
                rhs_scale=ws[c][:, first:end],
                start=(c == 0),
                stop=(c == CHUNKS - 1),
            )

        for j in EARLY:
            mx_pass(acc[j][:], j, 0, 0, COLS)
        regroup(1)
        quantise_chunk(1)
        quantise_x(0, 5, 6)
        for j in (7, 0, 1, 2, 3, 4, 6):
            mx_pass(acc[j][:], j, 1, 0, COLS)
        copy_out_single(nc.scalar.copy, 5, 2)
        copy_out_single(nc.vector.tensor_copy, 5, 3)
        for c in range(2, CHUNKS):
            regroup(c)
            g = c // 2
            if g < SLABS:
                if c % 2 == 0:
                    quantise_x(g, 4, 6)
                else:
                    move_by_one_column(g)
            quantise_chunk(c)
            if g < SLABS:
                if c % 2 == 1:
                    quantise_x(g, TILES, SLOTS)
                elif g >= 2:
                    quantise_x(g, 2, 4)
            if c < CHUNK_BY_CHUNK:
                for j in EARLY:
                    mx_pass(acc[j][:], j, c, 0, COLS)

        nc.vector.tensor_scalar(out=bias3[:], in0=bias1[:], scalar1=3.0, scalar2=None, op0=ALU.mult)
        nc.vector.tensor_scalar(out=bias_tile0[:], in0=bias1[:], scalar1=count0[:, 0:1], scalar2=None, op0=ALU.mult)
        nc.vector.tensor_scalar(out=bias_tile1[:], in0=bias1[:], scalar1=count1[:, 0:1], scalar2=None, op0=ALU.mult)

        out_rows = out.rearrange("(i j) c -> i j c", j=TILES)

        def finish(sums, j, first, end):
            summed = stage.tile([P, end - first], F32, tag="summed", name="summed%d_%d" % (j, first))
            nc.vector.tensor_tensor(out=summed[:], in0=sums, in1=bias_of.get(j, bias3)[:, first:end], op=ALU.add)
            result = keep.tile([P, end - first], F32, name="result%d_%d" % (j, first))
            nc.scalar.activation(out=result[:], in_=summed[:], func=ACT.Tanh)
            nc.sync.dma_start(out=out_rows[:, j, first:end], in_=result[:])

        for j in EARLY:
            for c in range(CHUNK_BY_CHUNK, CHUNKS):
                mx_pass(acc[j][:], j, c, 0, COLS)
            finish(acc[j][:], j, 0, COLS)
        for bank, first, end in LATE_GROUPS:
            late = psum.tile([P, end - first], F32, tag="bank%d" % bank, name="late%d" % first)
            for c in range(CHUNKS):
                mx_pass(late[:], LATE, c, first, end)
            finish(late[:], LATE, first, end)
